import numpy as np
import ml_dtypes


def mxq(x, axis, fmt="e4m3"):
    dtype, down = {"e4m3": (ml_dtypes.float8_e4m3fn, 7), "e5m2": (ml_dtypes.float8_e5m2, 14)}[fmt]
    v = np.moveaxis(np.asarray(x, np.float32).astype(ml_dtypes.bfloat16).astype(np.float64), axis, -1)
    blocks = v.reshape(v.shape[:-1] + (-1, 32))
    amax = np.abs(blocks).max(-1, keepdims=True)
    byte = np.maximum(np.where(amax > 0, np.frexp(amax)[1] - 1 + 127, 0) - down, 1)
    scale = np.exp2(byte - 127.0)
    codes = (blocks / scale).astype(np.float32).astype(dtype).astype(np.float64)
    return np.moveaxis((codes * scale).reshape(v.shape), -1, axis)


WIDE = False


def mx_kscale(k):
    if not WIDE:
        return np.ones(k)
    levels = np.array([10, -10, 5, -5, 0])
    a = np.random.permutation(np.resize(levels, k // 512 * 4)).reshape(k // 512, 4)
    idx = np.arange(k)
    return np.exp2(a[idx // 512, idx % 128 // 32])


BF16 = ml_dtypes.bfloat16


def bf(x):
    return np.asarray(x, np.float32).astype(BF16)


def f64(x):
    return np.asarray(x).astype(np.float64)


E2M1 = np.array([0.0, 0.5, 1.0, 1.5, 2.0, 3.0, 4.0, 6.0, -0.0, -0.5, -1.0, -1.5, -2.0, -3.0, -4.0, -6.0])


def pack_weight(w, fmt):
    k, n = w.shape
    w = f64(bf(w)).reshape(k // 32, 32, n)
    amax = np.abs(w).max(1)
    if fmt == "e4m3":
        byte = np.frexp(amax)[1] - 1 + 127 - 7
    else:
        mant, ex = np.frexp(amax / 6.0)
        byte = np.where(mant > 0.5, ex, ex - 1) + 127
    byte = np.clip(np.where(amax > 0, byte, 1), 1, 254)
    scaled = (w * np.exp2(127.0 - byte)[:, None, :]).reshape(k, n).astype(np.float32)
    by_word = np.ascontiguousarray(scaled.reshape(k // 512, 128, 4, n).transpose(0, 1, 3, 2))
    if fmt == "e4m3":
        words = by_word.astype(ml_dtypes.float8_e4m3fn).view(np.uint8)
    else:
        c = by_word.astype(ml_dtypes.float4_e2m1fn).view(np.uint8) & 0xF
        words = c[..., 0::2] | (c[..., 1::2] << 4)
    return np.ascontiguousarray(words), np.ascontiguousarray(byte.astype(np.uint8).reshape(k // 512, 16, n))


def unpack_weight(words, scales, fmt):
    g, p, n, _ = words.shape
    if fmt == "e4m3":
        vals = np.ascontiguousarray(words).view(ml_dtypes.float8_e4m3fn).astype(np.float64)
    else:
        nib = np.empty((g, p, n, 4), np.uint8)
        nib[..., 0::2] = words & 0xF
        nib[..., 1::2] = words >> 4
        vals = E2M1[nib]
    vals = vals * np.repeat(np.exp2(scales.astype(np.float64) - 127.0), 8, axis=1)[..., None]
    return vals.transpose(0, 1, 3, 2).reshape(g * 512, n)


B, C, MID, HH, WW = 1, 2048, 512, 32, 32
N = HH * WW


def setup_inputs():
    s, t = mx_kscale(N), mx_kscale(MID)
    a = np.exp(1.5 * np.random.standard_normal((B, N, N)))
    a = a / a.sum(-1, keepdims=True)
    attn = bf(a * s)
    h_x = bf(np.random.standard_normal((B, MID, N)) * 2.0 * t[:, None] / s)
    v_w = np.random.standard_normal((C, MID)) * 3.0 / np.sqrt(MID) / t
    v_w_words, v_w_scales = pack_weight(np.ascontiguousarray(v_w.T), "e4m3")
    return {
        "attn": attn,
        "h_x": h_x,
        "v_w_words": v_w_words,
        "v_w_scales": v_w_scales,
        "v_b": bf(np.random.standard_normal(C) * 0.3),
        "x": bf(np.random.standard_normal((B, C, HH, WW))),
    }


def reference(attn, h_x, v_w_words, v_w_scales, v_b, x):
    z = mxq(f64(h_x), 2, "e4m3") @ mxq(f64(attn), 2, "e4m3").transpose(0, 2, 1)
    y = (unpack_weight(v_w_words, v_w_scales, "e4m3").T @ mxq(z, 1, "e4m3")) + f64(v_b)[None, :, None]
    return y.reshape(B, C, HH, WW) + f64(x)

@@ -1,0 +1,159 @@
+from contextlib import ExitStack
+
+import concourse.mybir as mybir
+from concourse.masks import make_identity
+
+F32 = mybir.dt.float32
+BF16 = mybir.dt.bfloat16
+I32 = mybir.dt.int32
+U32 = mybir.dt.uint32
+U8 = mybir.dt.uint8
+FP8X4 = mybir.dt.float8_e4m3fn_x4
+ADD = mybir.AluOpType.add
+
+P = 128
+PACK = 4
+PAIR = 2
+POSITIONS = 1024
+MID = 512
+C_OUT = 2048
+PASSES = POSITIONS // (P * PACK)
+N_BLOCKS = POSITIONS // P
+N_HALF = 512
+HALVES = POSITIONS // N_HALF
+BLOCKS_PER_HALF = N_HALF // P
+O_TILES = C_OUT // P
+X_TILES_PER_LOAD = 2
+
+FLOPS = 2 * MID * POSITIONS * POSITIONS + 2 * C_OUT * MID * POSITIONS
+
+
+def tile_soablock_pb_kernel(tc, attn, h_x, v_w_words, v_w_scales, v_b, x, out):
+    nc = tc.nc
+    with ExitStack() as ctx:
+        keep = ctx.enter_context(tc.tile_pool(name="keep", bufs=1))
+        flipped_banks = ctx.enter_context(tc.psum_pool(name="flipped_banks", bufs=2))
+        z_banks = ctx.enter_context(tc.psum_pool(name="z_banks", bufs=2))
+        y_banks = ctx.enter_context(tc.psum_pool(name="y_banks", bufs=4))
+        ctx.enter_context(tc.manual_schedule())
+
+        h_rows = keep.tile([P, PACK, POSITIONS], BF16)
+        a_rows = keep.tile([P, N_BLOCKS, POSITIONS], BF16)
+        w_words = keep.tile([P, C_OUT], U32, align_bytes=64)
+        w_scales = keep.tile([P, C_OUT], U8, align_bytes=64)
+        x_rows = keep.tile([P, O_TILES, POSITIONS], BF16)
+        out_rows = keep.tile([P, O_TILES, POSITIONS], F32)
+        bias_rows = keep.tile([P, P], BF16)
+        bias_rows_f32 = keep.tile([P, P], F32)
+        bias = keep.tile([P, O_TILES], F32)
+        ident = keep.tile([P, P], F32)
+
+        h_grouped = keep.tile([P, PASSES, MID, PACK], BF16, align_bytes=64)
+        a_grouped = keep.tile([P, N_BLOCKS, PASSES, P, PACK], BF16, align_bytes=64)
+        z_grouped = keep.tile([P, POSITIONS, PACK], BF16, align_bytes=64)
+        h_codes = keep.tile([P, PASSES, MID], U32, align_bytes=64)
+        h_scales = keep.tile([P, PASSES, MID], U8, align_bytes=64)
+        a_codes = keep.tile([P, N_BLOCKS, PASSES, P], U32, align_bytes=64)
+        a_scales = keep.tile([P, N_BLOCKS, PASSES, P], U8, align_bytes=64)
+        z_codes = keep.tile([P, POSITIONS], U32, align_bytes=64)
+        z_scales = keep.tile([P, POSITIONS], U8, align_bytes=64)
+
+        x_view = x[0].rearrange("(i p) h w -> p i (h w)", p=P)
+        out_view = out[0].rearrange("(i p) h w -> p i (h w)", p=P)
+
+        nc.vector.memset(w_scales[:].bitcast(I32), 0)
+        nc.vector.memset(bias_rows[:], 0.0)
+        make_identity(nc, ident[:])
+
+        nc.scalar.dma_start(out=bias_rows[0:O_TILES, :], in_=v_b.rearrange("(i p) -> i p", p=P))
+        nc.sync.dma_start(out=h_rows[:], in_=h_x[0].rearrange("(p t) m -> p t m", t=PACK))
+        for j in range(N_BLOCKS):
+            nc.sync.dma_start(out=a_rows[:, j, :], in_=attn[0, j * P : (j + 1) * P, :])
+        for quadrant in range(4):
+            nc.sync.dma_start(
+                out=w_scales[32 * quadrant : 32 * quadrant + 4, :].bitcast(I32),
+                in_=v_w_scales[0, 4 * quadrant : 4 * quadrant + 4, :].bitcast(I32),
+            )
+        nc.sync.dma_start(
+            out=w_words[:].bitcast(I32), in_=v_w_words[0].rearrange("p o t -> p (o t)").bitcast(I32)
+        )
+        for first in range(0, O_TILES, X_TILES_PER_LOAD):
+            tiles = slice(first, first + X_TILES_PER_LOAD)
+            nc.sync.dma_start(out=x_rows[:, tiles, :], in_=x_view[:, tiles, :])
+
+        def flip_rows(rows, grouped, copy):
+            words = rows.bitcast(F32)
+            bank = flipped_banks.tile([P, PASSES, PAIR, P], F32)
+            for g in range(PASSES):
+                for u in range(PAIR):
+                    first_word = (PAIR * g + u) * P
+                    nc.tensor.transpose(bank[:, g, u, :], words[:, first_word : first_word + P], ident[:])
+            copy(out=grouped.bitcast(F32), in_=bank[:].rearrange("p g u r -> p g r u"))
+
+        for t in range(PACK):
+            flip_rows(h_rows[:, t, :], h_grouped[:, :, t * P : (t + 1) * P, :], nc.vector.tensor_copy)
+        nc.vector.quantize_mx(
+            out=h_codes[:].rearrange("p g c -> p (g c)").bitcast(FP8X4),
+            scales=h_scales[:].rearrange("p g c -> p (g c)"),
+            in_=h_grouped[:].rearrange("p g c t -> p (g c t)"),
+        )
+        nc.vector.tensor_copy(out=bias_rows_f32[:], in_=bias_rows[:])
+
+        for half in range(HALVES):
+            blocks = range(half * BLOCKS_PER_HALF, (half + 1) * BLOCKS_PER_HALF)
+            for j in blocks:
+                flip_rows(a_rows[:, j, :], a_grouped[:, j], nc.scalar.copy)
+                nc.vector.quantize_mx(
+                    out=a_codes[:, j].rearrange("p g r -> p (g r)").bitcast(FP8X4),
+                    scales=a_scales[:, j].rearrange("p g r -> p (g r)"),
+                    in_=a_grouped[:, j].rearrange("p g r t -> p (g r t)"),
+                )
+            if half == 0:
+                bias_bank = flipped_banks.tile([P, PASSES, PAIR, P], F32, tag="bank")
+                nc.tensor.transpose(bias_bank[:, 0, 0, :], bias_rows_f32[:], ident[:])
+                nc.vector.tensor_copy(out=bias[:], in_=bias_bank[:, 0, 0, 0:O_TILES])
+            for j in blocks:
+                z_bank = z_banks.tile([P, PACK, P], F32)
+                for t in range(PACK):
+                    for g in range(PASSES):
+                        nc.tensor.matmul_mx(
+                            out=z_bank[:, t, :],
+                            lhsT=h_codes[:, g, t * P : (t + 1) * P].bitcast(FP8X4),
+                            lhsT_scale=h_scales[:, g, t * P : (t + 1) * P],
+                            rhs=a_codes[:, j, g, :].bitcast(FP8X4),
+                            rhs_scale=a_scales[:, j, g, :],
+                            start=(g == 0),
+                            stop=(g == PASSES - 1),
+                        )
+                copy = nc.vector.tensor_copy if j % 2 == 0 else nc.scalar.copy
+                copy(out=z_grouped[:, j * P : (j + 1) * P, :], in_=z_bank[:].rearrange("p t r -> p r t"))
+            cols = slice(half * N_HALF, (half + 1) * N_HALF)
+            nc.vector.quantize_mx(
+                out=z_codes[:, cols].bitcast(FP8X4),
+                scales=z_scales[:, cols],
+                in_=z_grouped[:, cols, :].rearrange("p n t -> p (n t)"),
+            )
+
+        for i in range(O_TILES):
+            channels = slice(i * P, (i + 1) * P)
+            for half in range(HALVES):
+                cols = slice(half * N_HALF, (half + 1) * N_HALF)
+                y_bank = y_banks.tile([P, N_HALF], F32)
+                nc.tensor.matmul_mx(
+                    out=y_bank[:],
+                    lhsT=w_words[:, channels].bitcast(FP8X4),
+                    lhsT_scale=w_scales[:, channels],
+                    rhs=z_codes[:, cols].bitcast(FP8X4),
+                    rhs_scale=z_scales[:, cols],
+                    start=True,
+                    stop=True,
+                )
+                nc.vector.scalar_tensor_tensor(
+                    out=out_rows[:, i, cols],
+                    in0=y_bank[:],
+                    scalar=bias[:, i : i + 1],
+                    in1=x_rows[:, i, cols],
+                    op0=ADD,
+                    op1=ADD,
+                )
+            nc.sync.dma_start(out=out_view[:, i, :], in_=out_rows[:, i, :])

@@ -10,6 +10,7 @@ U32 = mybir.dt.uint32
 U8 = mybir.dt.uint8
 FP8X4 = mybir.dt.float8_e4m3fn_x4
 ADD = mybir.AluOpType.add
+IDENTITY = mybir.ActivationFunctionType.Identity
 
 P = 128
 PACK = 4
@@ -19,9 +20,9 @@ MID = 512
 C_OUT = 2048
 PASSES = POSITIONS // (P * PACK)
 N_BLOCKS = POSITIONS // P
+STEP = 2
 N_HALF = 512
 HALVES = POSITIONS // N_HALF
-BLOCKS_PER_HALF = N_HALF // P
 O_TILES = C_OUT // P
 X_TILES_PER_LOAD = 2
 
@@ -32,9 +33,9 @@ def tile_soablock_pb_kernel(tc, attn, h_x, v_w_words, v_w_scales, v_b, x, out):
     nc = tc.nc
     with ExitStack() as ctx:
         keep = ctx.enter_context(tc.tile_pool(name="keep", bufs=1))
-        flipped_banks = ctx.enter_context(tc.psum_pool(name="flipped_banks", bufs=2))
+        flipped_banks = ctx.enter_context(tc.psum_pool(name="flipped_banks", bufs=3))
         z_banks = ctx.enter_context(tc.psum_pool(name="z_banks", bufs=2))
-        y_banks = ctx.enter_context(tc.psum_pool(name="y_banks", bufs=4))
+        y_banks = ctx.enter_context(tc.psum_pool(name="y_banks", bufs=3))
         ctx.enter_context(tc.manual_schedule())
 
         h_rows = keep.tile([P, PACK, POSITIONS], BF16)
@@ -48,25 +49,27 @@ def tile_soablock_pb_kernel(tc, attn, h_x, v_w_words, v_w_scales, v_b, x, out):
         bias = keep.tile([P, O_TILES], F32)
         ident = keep.tile([P, P], F32)
 
-        h_grouped = keep.tile([P, PASSES, MID, PACK], BF16, align_bytes=64)
+        h_grouped = keep.tile([P, PACK, PASSES, P, PACK], BF16, align_bytes=64)
         a_grouped = keep.tile([P, N_BLOCKS, PASSES, P, PACK], BF16, align_bytes=64)
         z_grouped = keep.tile([P, POSITIONS, PACK], BF16, align_bytes=64)
-        h_codes = keep.tile([P, PASSES, MID], U32, align_bytes=64)
-        h_scales = keep.tile([P, PASSES, MID], U8, align_bytes=64)
+        h_codes = keep.tile([P, PACK, PASSES, P], U32, align_bytes=64)
+        h_scales = keep.tile([P, PACK, PASSES, P], U8, align_bytes=64)
         a_codes = keep.tile([P, N_BLOCKS, PASSES, P], U32, align_bytes=64)
         a_scales = keep.tile([P, N_BLOCKS, PASSES, P], U8, align_bytes=64)
         z_codes = keep.tile([P, POSITIONS], U32, align_bytes=64)
         z_scales = keep.tile([P, POSITIONS], U8, align_bytes=64)
 
+        h_view = h_x[0].rearrange("(p t) m -> p t m", t=PACK)
         x_view = x[0].rearrange("(i p) h w -> p i (h w)", p=P)
         out_view = out[0].rearrange("(i p) h w -> p i (h w)", p=P)
 
-        nc.vector.memset(w_scales[:].bitcast(I32), 0)
         nc.vector.memset(bias_rows[:], 0.0)
+        nc.vector.memset(w_scales[:].bitcast(I32), 0)
         make_identity(nc, ident[:])
 
-        nc.scalar.dma_start(out=bias_rows[0:O_TILES, :], in_=v_b.rearrange("(i p) -> i p", p=P))
-        nc.sync.dma_start(out=h_rows[:], in_=h_x[0].rearrange("(p t) m -> p t m", t=PACK))
+        nc.sync.dma_start(out=bias_rows[0:O_TILES, :], in_=v_b.rearrange("(i p) -> i p", p=P))
+        for t in range(PACK):
+            nc.sync.dma_start(out=h_rows[:, t, :], in_=h_view[:, t, :])
         for j in range(N_BLOCKS):
             nc.sync.dma_start(out=a_rows[:, j, :], in_=attn[0, j * P : (j + 1) * P, :])
         for quadrant in range(4):
@@ -81,58 +84,67 @@ def tile_soablock_pb_kernel(tc, attn, h_x, v_w_words, v_w_scales, v_b, x, out):
             tiles = slice(first, first + X_TILES_PER_LOAD)
             nc.sync.dma_start(out=x_rows[:, tiles, :], in_=x_view[:, tiles, :])
 
-        def flip_rows(rows, grouped, copy):
-            words = rows.bitcast(F32)
-            bank = flipped_banks.tile([P, PASSES, PAIR, P], F32)
-            for g in range(PASSES):
-                for u in range(PAIR):
-                    first_word = (PAIR * g + u) * P
-                    nc.tensor.transpose(bank[:, g, u, :], words[:, first_word : first_word + P], ident[:])
-            copy(out=grouped.bitcast(F32), in_=bank[:].rearrange("p g u r -> p g r u"))
-
-        for t in range(PACK):
-            flip_rows(h_rows[:, t, :], h_grouped[:, :, t * P : (t + 1) * P, :], nc.vector.tensor_copy)
-        nc.vector.quantize_mx(
-            out=h_codes[:].rearrange("p g c -> p (g c)").bitcast(FP8X4),
-            scales=h_scales[:].rearrange("p g c -> p (g c)"),
-            in_=h_grouped[:].rearrange("p g c t -> p (g c t)"),
-        )
         nc.vector.tensor_copy(out=bias_rows_f32[:], in_=bias_rows[:])
+        bias_bank = flipped_banks.tile([P, PASSES, PAIR, P], F32, tag="bank")
+        nc.tensor.transpose(bias_bank[:, 0, 0, :], bias_rows_f32[:], ident[:])
+        nc.vector.tensor_copy(out=bias[:], in_=bias_bank[:, 0, 0, 0:O_TILES])
 
-        for half in range(HALVES):
-            blocks = range(half * BLOCKS_PER_HALF, (half + 1) * BLOCKS_PER_HALF)
-            for j in blocks:
-                flip_rows(a_rows[:, j, :], a_grouped[:, j], nc.scalar.copy)
-                nc.vector.quantize_mx(
-                    out=a_codes[:, j].rearrange("p g r -> p (g r)").bitcast(FP8X4),
-                    scales=a_scales[:, j].rearrange("p g r -> p (g r)"),
-                    in_=a_grouped[:, j].rearrange("p g r t -> p (g r t)"),
-                )
-            if half == 0:
-                bias_bank = flipped_banks.tile([P, PASSES, PAIR, P], F32, tag="bank")
-                nc.tensor.transpose(bias_bank[:, 0, 0, :], bias_rows_f32[:], ident[:])
-                nc.vector.tensor_copy(out=bias[:], in_=bias_bank[:, 0, 0, 0:O_TILES])
-            for j in blocks:
+        def flip(rows, grouped, first):
+            for b in range(first, first + STEP):
+                words = rows[:, b, :].bitcast(F32)
+                bank = flipped_banks.tile([P, PASSES, PAIR, P], F32)
+                for g in range(PASSES):
+                    for u in range(PAIR):
+                        first_word = (PAIR * g + u) * P
+                        nc.tensor.transpose(bank[:, g, u, :], words[:, first_word : first_word + P], ident[:])
+                copy = nc.vector.tensor_copy if b % 2 == 0 else nc.scalar.copy
+                copy(out=grouped[:, b].bitcast(F32), in_=bank[:].rearrange("p g u r -> p g r u"))
+
+        def quantise(grouped, codes, scales, first):
+            blocks = slice(first, first + STEP)
+            nc.vector.quantize_mx(
+                out=codes[:, blocks].rearrange("p b g r -> p (b g r)").bitcast(FP8X4),
+                scales=scales[:, blocks].rearrange("p b g r -> p (b g r)"),
+                in_=grouped[:, blocks].rearrange("p b g r t -> p (b g r t)"),
+            )
+
+        def multiply(first):
+            for j in range(first, first + STEP):
                 z_bank = z_banks.tile([P, PACK, P], F32)
                 for t in range(PACK):
                     for g in range(PASSES):
                         nc.tensor.matmul_mx(
                             out=z_bank[:, t, :],
-                            lhsT=h_codes[:, g, t * P : (t + 1) * P].bitcast(FP8X4),
-                            lhsT_scale=h_scales[:, g, t * P : (t + 1) * P],
+                            lhsT=h_codes[:, t, g, :].bitcast(FP8X4),
+                            lhsT_scale=h_scales[:, t, g, :],
                             rhs=a_codes[:, j, g, :].bitcast(FP8X4),
                             rhs_scale=a_scales[:, j, g, :],
                             start=(g == 0),
                             stop=(g == PASSES - 1),
                         )
-                copy = nc.vector.tensor_copy if j % 2 == 0 else nc.scalar.copy
-                copy(out=z_grouped[:, j * P : (j + 1) * P, :], in_=z_bank[:].rearrange("p t r -> p r t"))
-            cols = slice(half * N_HALF, (half + 1) * N_HALF)
+                nc.scalar.copy(out=z_grouped[:, j * P : (j + 1) * P, :], in_=z_bank[:].rearrange("p t r -> p r t"))
+
+        def quantise_z(first):
+            cols = slice(first * P, (first + STEP) * P)
             nc.vector.quantize_mx(
                 out=z_codes[:, cols].bitcast(FP8X4),
                 scales=z_scales[:, cols],
                 in_=z_grouped[:, cols, :].rearrange("p n t -> p (n t)"),
             )
+
+        for first in range(0, PACK, STEP):
+            flip(h_rows, h_grouped, first)
+        for first in range(0, PACK, STEP):
+            quantise(h_grouped, h_codes, h_scales, first)
+
+        for first in range(0, N_BLOCKS + 2 * STEP, STEP):
+            if first < N_BLOCKS:
+                flip(a_rows, a_grouped, first)
+                quantise(a_grouped, a_codes, a_scales, first)
+            if STEP <= first < N_BLOCKS + STEP:
+                multiply(first - STEP)
+            if first >= 2 * STEP:
+                quantise_z(first - 2 * STEP)
 
         for i in range(O_TILES):
             channels = slice(i * P, (i + 1) * P)
@@ -148,12 +160,20 @@ def tile_soablock_pb_kernel(tc, attn, h_x, v_w_words, v_w_scales, v_b, x, out):
                     start=True,
                     stop=True,
                 )
-                nc.vector.scalar_tensor_tensor(
-                    out=out_rows[:, i, cols],
-                    in0=y_bank[:],
-                    scalar=bias[:, i : i + 1],
-                    in1=x_rows[:, i, cols],
-                    op0=ADD,
-                    op1=ADD,
-                )
+                if i % 2 == 1 and half == 1:
+                    nc.scalar.activation(
+                        out=out_rows[:, i, cols], in_=y_bank[:], func=IDENTITY, bias=bias[:, i : i + 1]
+                    )
+                    nc.gpsimd.tensor_tensor(
+                        out=out_rows[:, i, cols], in0=out_rows[:, i, cols], in1=x_rows[:, i, cols], op=ADD
+                    )
+                else:
+                    nc.vector.scalar_tensor_tensor(
+                        out=out_rows[:, i, cols],
+                        in0=y_bank[:],
+                        scalar=bias[:, i : i + 1],
+                        in1=x_rows[:, i, cols],
+                        op0=ADD,
+                        op1=ADD,
+                    )
             nc.sync.dma_start(out=out_view[:, i, :], in_=out_rows[:, i, :])

@@ -33,9 +33,7 @@ def tile_soablock_pb_kernel(tc, attn, h_x, v_w_words, v_w_scales, v_b, x, out):
     nc = tc.nc
     with ExitStack() as ctx:
         keep = ctx.enter_context(tc.tile_pool(name="keep", bufs=1))
-        flipped_banks = ctx.enter_context(tc.psum_pool(name="flipped_banks", bufs=3))
-        z_banks = ctx.enter_context(tc.psum_pool(name="z_banks", bufs=2))
-        y_banks = ctx.enter_context(tc.psum_pool(name="y_banks", bufs=3))
+        banks = ctx.enter_context(tc.psum_pool(name="banks", bufs=8))
         ctx.enter_context(tc.manual_schedule())
 
         h_rows = keep.tile([P, PACK, POSITIONS], BF16)
@@ -45,9 +43,9 @@ def tile_soablock_pb_kernel(tc, attn, h_x, v_w_words, v_w_scales, v_b, x, out):
         x_rows = keep.tile([P, O_TILES, POSITIONS], BF16)
         out_rows = keep.tile([P, O_TILES, POSITIONS], F32)
         bias_rows = keep.tile([P, P], BF16)
-        bias_rows_f32 = keep.tile([P, P], F32)
         bias = keep.tile([P, O_TILES], F32)
         ident = keep.tile([P, P], F32)
+        ident_bf16 = keep.tile([P, P], BF16)
 
         h_grouped = keep.tile([P, PACK, PASSES, P, PACK], BF16, align_bytes=64)
         a_grouped = keep.tile([P, N_BLOCKS, PASSES, P, PACK], BF16, align_bytes=64)
@@ -66,8 +64,9 @@ def tile_soablock_pb_kernel(tc, attn, h_x, v_w_words, v_w_scales, v_b, x, out):
         nc.vector.memset(bias_rows[:], 0.0)
         nc.vector.memset(w_scales[:].bitcast(I32), 0)
         make_identity(nc, ident[:])
+        make_identity(nc, ident_bf16[:])
 
-        nc.sync.dma_start(out=bias_rows[0:O_TILES, :], in_=v_b.rearrange("(i p) -> i p", p=P))
+        nc.scalar.dma_start(out=bias_rows[0:O_TILES, :], in_=v_b.rearrange("(i p) -> i p", p=P))
         for t in range(PACK):
             nc.sync.dma_start(out=h_rows[:, t, :], in_=h_view[:, t, :])
         for j in range(N_BLOCKS):
@@ -84,21 +83,16 @@ def tile_soablock_pb_kernel(tc, attn, h_x, v_w_words, v_w_scales, v_b, x, out):
             tiles = slice(first, first + X_TILES_PER_LOAD)
             nc.sync.dma_start(out=x_rows[:, tiles, :], in_=x_view[:, tiles, :])
 
-        nc.vector.tensor_copy(out=bias_rows_f32[:], in_=bias_rows[:])
-        bias_bank = flipped_banks.tile([P, PASSES, PAIR, P], F32, tag="bank")
-        nc.tensor.transpose(bias_bank[:, 0, 0, :], bias_rows_f32[:], ident[:])
-        nc.vector.tensor_copy(out=bias[:], in_=bias_bank[:, 0, 0, 0:O_TILES])
-
         def flip(rows, grouped, first):
             for b in range(first, first + STEP):
                 words = rows[:, b, :].bitcast(F32)
-                bank = flipped_banks.tile([P, PASSES, PAIR, P], F32)
+                flipped = banks.tile([P, PASSES, PAIR, P], F32, tag="bank")
                 for g in range(PASSES):
                     for u in range(PAIR):
                         first_word = (PAIR * g + u) * P
-                        nc.tensor.transpose(bank[:, g, u, :], words[:, first_word : first_word + P], ident[:])
+                        nc.tensor.transpose(flipped[:, g, u, :], words[:, first_word : first_word + P], ident[:])
                 copy = nc.vector.tensor_copy if b % 2 == 0 else nc.scalar.copy
-                copy(out=grouped[:, b].bitcast(F32), in_=bank[:].rearrange("p g u r -> p g r u"))
+                copy(out=grouped[:, b].bitcast(F32), in_=flipped[:].rearrange("p g u r -> p g r u"))
 
         def quantise(grouped, codes, scales, first):
             blocks = slice(first, first + STEP)
@@ -110,7 +104,7 @@ def tile_soablock_pb_kernel(tc, attn, h_x, v_w_words, v_w_scales, v_b, x, out):
 
         def multiply(first):
             for j in range(first, first + STEP):
-                z_bank = z_banks.tile([P, PACK, P], F32)
+                z_bank = banks.tile([P, PACK, P], F32, tag="bank")
                 for t in range(PACK):
                     for g in range(PASSES):
                         nc.tensor.matmul_mx(
@@ -137,6 +131,10 @@ def tile_soablock_pb_kernel(tc, attn, h_x, v_w_words, v_w_scales, v_b, x, out):
         for first in range(0, PACK, STEP):
             quantise(h_grouped, h_codes, h_scales, first)
 
+        bias_bank = banks.tile([P, P], BF16, tag="bank")
+        nc.tensor.transpose(bias_bank[:], bias_rows[:], ident_bf16[:])
+        nc.vector.tensor_copy(out=bias[:], in_=bias_bank[:, 0:O_TILES])
+
         for first in range(0, N_BLOCKS + 2 * STEP, STEP):
             if first < N_BLOCKS:
                 flip(a_rows, a_grouped, first)
@@ -150,7 +148,7 @@ def tile_soablock_pb_kernel(tc, attn, h_x, v_w_words, v_w_scales, v_b, x, out):
             channels = slice(i * P, (i + 1) * P)
             for half in range(HALVES):
                 cols = slice(half * N_HALF, (half + 1) * N_HALF)
-                y_bank = y_banks.tile([P, N_HALF], F32)
+                y_bank = banks.tile([P, N_HALF], F32, tag="bank")
                 nc.tensor.matmul_mx(
                     out=y_bank[:],
                     lhsT=w_words[:, channels].bitcast(FP8X4),

@@ -24,6 +24,9 @@ STEP = 2
 N_HALF = 512
 HALVES = POSITIONS // N_HALF
 O_TILES = C_OUT // P
+LIVE = 4
+PLANES = 4
+TILES_PER_PLANE = O_TILES // PLANES
 X_TILES_PER_LOAD = 2
 
 FLOPS = 2 * MID * POSITIONS * POSITIONS + 2 * C_OUT * MID * POSITIONS
@@ -39,7 +42,7 @@ def tile_soablock_pb_kernel(tc, attn, h_x, v_w_words, v_w_scales, v_b, x, out):
         h_rows = keep.tile([P, PACK, POSITIONS], BF16)
         a_rows = keep.tile([P, N_BLOCKS, POSITIONS], BF16)
         w_words = keep.tile([P, C_OUT], U32, align_bytes=64)
-        w_scales = keep.tile([P, C_OUT], U8, align_bytes=64)
+        w_planes = keep.tile([P, C_OUT // PLANES], U8, align_bytes=64)
         x_rows = keep.tile([P, O_TILES, POSITIONS], BF16)
         out_rows = keep.tile([P, O_TILES, POSITIONS], F32)
         bias_rows = keep.tile([P, P], BF16)
@@ -62,7 +65,7 @@ def tile_soablock_pb_kernel(tc, attn, h_x, v_w_words, v_w_scales, v_b, x, out):
         out_view = out[0].rearrange("(i p) h w -> p i (h w)", p=P)
 
         nc.vector.memset(bias_rows[:], 0.0)
-        nc.vector.memset(w_scales[:].bitcast(I32), 0)
+        nc.vector.memset(w_planes[:].bitcast(I32), 0)
         make_identity(nc, ident[:])
         make_identity(nc, ident_bf16[:])
 
@@ -71,10 +74,11 @@ def tile_soablock_pb_kernel(tc, attn, h_x, v_w_words, v_w_scales, v_b, x, out):
             nc.sync.dma_start(out=h_rows[:, t, :], in_=h_view[:, t, :])
         for j in range(N_BLOCKS):
             nc.sync.dma_start(out=a_rows[:, j, :], in_=attn[0, j * P : (j + 1) * P, :])
-        for quadrant in range(4):
+        scale_rows = v_w_scales[0].rearrange("(quadrant r) (k c) -> quadrant k r c", r=LIVE, k=PLANES)
+        for quadrant in range(P // 32):
             nc.sync.dma_start(
-                out=w_scales[32 * quadrant : 32 * quadrant + 4, :].bitcast(I32),
-                in_=v_w_scales[0, 4 * quadrant : 4 * quadrant + 4, :].bitcast(I32),
+                out=w_planes[32 * quadrant : 32 * quadrant + PLANES * LIVE, :].bitcast(I32),
+                in_=scale_rows[quadrant].bitcast(I32),
             )
         nc.sync.dma_start(
             out=w_words[:].bitcast(I32), in_=v_w_words[0].rearrange("p o t -> p (o t)").bitcast(I32)
@@ -146,13 +150,15 @@ def tile_soablock_pb_kernel(tc, attn, h_x, v_w_words, v_w_scales, v_b, x, out):
 
         for i in range(O_TILES):
             channels = slice(i * P, (i + 1) * P)
+            plane_top = LIVE * (i // TILES_PER_PLANE)
+            plane_cols = slice((i % TILES_PER_PLANE) * P, (i % TILES_PER_PLANE + 1) * P)
             for half in range(HALVES):
                 cols = slice(half * N_HALF, (half + 1) * N_HALF)
                 y_bank = banks.tile([P, N_HALF], F32, tag="bank")
                 nc.tensor.matmul_mx(
                     out=y_bank[:],
                     lhsT=w_words[:, channels].bitcast(FP8X4),
-                    lhsT_scale=w_scales[:, channels],
+                    lhsT_scale=w_planes[plane_top:P, plane_cols],
                     rhs=z_codes[:, cols].bitcast(FP8X4),
                     rhs_scale=z_scales[:, cols],
                     start=True,

@@ -28,6 +28,7 @@ LIVE = 4
 PLANES = 4
 TILES_PER_PLANE = O_TILES // PLANES
 X_TILES_PER_LOAD = 2
+EARLY = 4
 
 FLOPS = 2 * MID * POSITIONS * POSITIONS + 2 * C_OUT * MID * POSITIONS
 
@@ -139,45 +140,59 @@ def tile_soablock_pb_kernel(tc, attn, h_x, v_w_words, v_w_scales, v_b, x, out):
         nc.tensor.transpose(bias_bank[:], bias_rows[:], ident_bf16[:])
         nc.vector.tensor_copy(out=bias[:], in_=bias_bank[:, 0:O_TILES])
 
-        for first in range(0, N_BLOCKS + 2 * STEP, STEP):
+        def produce(i, half):
+            channels = slice(i * P, (i + 1) * P)
+            plane_top = LIVE * (i // TILES_PER_PLANE)
+            plane_cols = slice((i % TILES_PER_PLANE) * P, (i % TILES_PER_PLANE + 1) * P)
+            cols = slice(half * N_HALF, (half + 1) * N_HALF)
+            y_bank = banks.tile([P, N_HALF], F32, tag="bank")
+            nc.tensor.matmul_mx(
+                out=y_bank[:],
+                lhsT=w_words[:, channels].bitcast(FP8X4),
+                lhsT_scale=w_planes[plane_top:P, plane_cols],
+                rhs=z_codes[:, cols].bitcast(FP8X4),
+                rhs_scale=z_scales[:, cols],
+                start=True,
+                stop=True,
+            )
+            if i % 2 == 1 and half == 1:
+                nc.scalar.activation(out=out_rows[:, i, cols], in_=y_bank[:], func=IDENTITY, bias=bias[:, i : i + 1])
+                nc.gpsimd.tensor_tensor(
+                    out=out_rows[:, i, cols], in0=out_rows[:, i, cols], in1=x_rows[:, i, cols], op=ADD
+                )
+            else:
+                nc.vector.scalar_tensor_tensor(
+                    out=out_rows[:, i, cols],
+                    in0=y_bank[:],
+                    scalar=bias[:, i : i + 1],
+                    in1=x_rows[:, i, cols],
+                    op0=ADD,
+                    op1=ADD,
+                )
+
+        def store_half(i, half):
+            cols = slice(half * N_HALF, (half + 1) * N_HALF)
+            nc.sync.dma_start(out=out_view[:, i, cols], in_=out_rows[:, i, cols])
+
+        for first in range(0, N_BLOCKS + STEP, STEP):
             if first < N_BLOCKS:
                 flip(a_rows, a_grouped, first)
                 quantise(a_grouped, a_codes, a_scales, first)
-            if STEP <= first < N_BLOCKS + STEP:
+            if STEP <= first:
                 multiply(first - STEP)
             if first >= 2 * STEP:
                 quantise_z(first - 2 * STEP)
 
-        for i in range(O_TILES):
-            channels = slice(i * P, (i + 1) * P)
-            plane_top = LIVE * (i // TILES_PER_PLANE)
-            plane_cols = slice((i % TILES_PER_PLANE) * P, (i % TILES_PER_PLANE + 1) * P)
+        for i in range(EARLY):
+            if i == EARLY // 2:
+                quantise_z(N_BLOCKS - STEP)
+            produce(i, 0)
+            store_half(i, 0)
+        for i in range(EARLY):
+            produce(i, 1)
+            store_half(i, 1)
+
+        for i in range(EARLY, O_TILES):
             for half in range(HALVES):
-                cols = slice(half * N_HALF, (half + 1) * N_HALF)
-                y_bank = banks.tile([P, N_HALF], F32, tag="bank")
-                nc.tensor.matmul_mx(
-                    out=y_bank[:],
-                    lhsT=w_words[:, channels].bitcast(FP8X4),
-                    lhsT_scale=w_planes[plane_top:P, plane_cols],
-                    rhs=z_codes[:, cols].bitcast(FP8X4),
-                    rhs_scale=z_scales[:, cols],
-                    start=True,
-                    stop=True,
-                )
-                if i % 2 == 1 and half == 1:
-                    nc.scalar.activation(
-                        out=out_rows[:, i, cols], in_=y_bank[:], func=IDENTITY, bias=bias[:, i : i + 1]
-                    )
-                    nc.gpsimd.tensor_tensor(
-                        out=out_rows[:, i, cols], in0=out_rows[:, i, cols], in1=x_rows[:, i, cols], op=ADD
-                    )
-                else:
-                    nc.vector.scalar_tensor_tensor(
-                        out=out_rows[:, i, cols],
-                        in0=y_bank[:],
-                        scalar=bias[:, i : i + 1],
-                        in1=x_rows[:, i, cols],
-                        op0=ADD,
-                        op1=ADD,
-                    )
+                produce(i, half)
             nc.sync.dma_start(out=out_view[:, i, :], in_=out_rows[:, i, :])

@@ -62,6 +62,7 @@ def tile_soablock_pb_kernel(tc, attn, h_x, v_w_words, v_w_scales, v_b, x, out):
         z_scales = keep.tile([P, POSITIONS], U8, align_bytes=64)
 
         h_view = h_x[0].rearrange("(p t) m -> p t m", t=PACK)
+        a_view = attn[0].rearrange("(half p c) m -> p half c m", half=HALVES, p=P)
         x_view = x[0].rearrange("(i p) h w -> p i (h w)", p=P)
         out_view = out[0].rearrange("(i p) h w -> p i (h w)", p=P)
 
@@ -71,10 +72,11 @@ def tile_soablock_pb_kernel(tc, attn, h_x, v_w_words, v_w_scales, v_b, x, out):
         make_identity(nc, ident_bf16[:])
 
         nc.scalar.dma_start(out=bias_rows[0:O_TILES, :], in_=v_b.rearrange("(i p) -> i p", p=P))
-        for t in range(PACK):
-            nc.sync.dma_start(out=h_rows[:, t, :], in_=h_view[:, t, :])
-        for j in range(N_BLOCKS):
-            nc.sync.dma_start(out=a_rows[:, j, :], in_=attn[0, j * P : (j + 1) * P, :])
+        for first in range(0, PACK, STEP):
+            nc.sync.dma_start(out=h_rows[:, first : first + STEP, :], in_=h_view[:, first : first + STEP, :])
+        for first in range(0, N_BLOCKS, STEP):
+            half, c = divmod(first, N_BLOCKS // HALVES)
+            nc.sync.dma_start(out=a_rows[:, first : first + STEP, :], in_=a_view[:, half, c : c + STEP, :])
         scale_rows = v_w_scales[0].rearrange("(quadrant r) (k c) -> quadrant k r c", r=LIVE, k=PLANES)
         for quadrant in range(P // 32):
             nc.sync.dma_start(
@@ -146,6 +148,8 @@ def tile_soablock_pb_kernel(tc, attn, h_x, v_w_words, v_w_scales, v_b, x, out):
             plane_cols = slice((i % TILES_PER_PLANE) * P, (i % TILES_PER_PLANE + 1) * P)
             cols = slice(half * N_HALF, (half + 1) * N_HALF)
             y_bank = banks.tile([P, N_HALF], F32, tag="bank")
+            y_by_n = y_bank[:].rearrange("p (c r) -> p r c", r=P)
+            out_by_n = out_rows[:, i, cols].rearrange("p (r c) -> p r c", r=P)
             nc.tensor.matmul_mx(
                 out=y_bank[:],
                 lhsT=w_words[:, channels].bitcast(FP8X4),
@@ -156,16 +160,16 @@ def tile_soablock_pb_kernel(tc, attn, h_x, v_w_words, v_w_scales, v_b, x, out):
                 stop=True,
             )
             if i % 2 == 1 and half == 1:
-                nc.scalar.activation(out=out_rows[:, i, cols], in_=y_bank[:], func=IDENTITY, bias=bias[:, i : i + 1])
+                nc.scalar.activation(out=out_by_n, in_=y_by_n, func=IDENTITY, bias=bias[:, i : i + 1])
                 nc.gpsimd.tensor_tensor(
                     out=out_rows[:, i, cols], in0=out_rows[:, i, cols], in1=x_rows[:, i, cols], op=ADD
                 )
             else:
                 nc.vector.scalar_tensor_tensor(
-                    out=out_rows[:, i, cols],
-                    in0=y_bank[:],
+                    out=out_by_n,
+                    in0=y_by_n,
                     scalar=bias[:, i : i + 1],
-                    in1=x_rows[:, i, cols],
+                    in1=x_rows[:, i, cols].rearrange("p (r c) -> p r c", r=P),
                     op0=ADD,
                     op1=ADD,
                 )

@@ -27,7 +27,9 @@ O_TILES = C_OUT // P
 LIVE = 4
 PLANES = 4
 TILES_PER_PLANE = O_TILES // PLANES
+CHUNKS = PLANES
 X_TILES_PER_LOAD = 2
+OUT_TILES_PER_STORE = 2
 EARLY = 4
 
 FLOPS = 2 * MID * POSITIONS * POSITIONS + 2 * C_OUT * MID * POSITIONS
@@ -42,11 +44,13 @@ def tile_soablock_pb_kernel(tc, attn, h_x, v_w_words, v_w_scales, v_b, x, out):
 
         h_rows = keep.tile([P, PACK, POSITIONS], BF16)
         a_rows = keep.tile([P, N_BLOCKS, POSITIONS], BF16)
-        w_words = keep.tile([P, C_OUT], U32, align_bytes=64)
-        w_planes = keep.tile([P, C_OUT // PLANES], U8, align_bytes=64)
+        w_loaded = keep.tile([P, C_OUT], U32, align_bytes=64)
+        w_words = keep.tile([P, CHUNKS - 1, TILES_PER_PLANE, P], U32, align_bytes=64)
+        s_loaded = keep.tile([P, C_OUT // PLANES], U8, align_bytes=64)
+        w_planes = keep.tile([P, TILES_PER_PLANE, P], U8, align_bytes=64)
         x_rows = keep.tile([P, O_TILES, POSITIONS], BF16)
         out_rows = keep.tile([P, O_TILES, POSITIONS], F32)
-        bias_rows = keep.tile([P, P], BF16)
+        bias_rows = keep.tile([P, C_OUT // CHUNKS], BF16)
         bias = keep.tile([P, O_TILES], F32)
         ident = keep.tile([P, P], F32)
         ident_bf16 = keep.tile([P, P], BF16)
@@ -65,13 +69,15 @@ def tile_soablock_pb_kernel(tc, attn, h_x, v_w_words, v_w_scales, v_b, x, out):
         a_view = attn[0].rearrange("(half p c) m -> p half c m", half=HALVES, p=P)
         x_view = x[0].rearrange("(i p) h w -> p i (h w)", p=P)
         out_view = out[0].rearrange("(i p) h w -> p i (h w)", p=P)
+        x_chunks = x[0].rearrange("(k p e) h w -> p k e (h w)", k=CHUNKS, p=P)
+        out_chunks = out[0].rearrange("(k p e) h w -> p k e (h w)", k=CHUNKS, p=P)
 
         nc.vector.memset(bias_rows[:], 0.0)
-        nc.vector.memset(w_planes[:].bitcast(I32), 0)
+        nc.vector.memset(s_loaded[:].bitcast(I32), 0)
         make_identity(nc, ident[:])
         make_identity(nc, ident_bf16[:])
 
-        nc.scalar.dma_start(out=bias_rows[0:O_TILES, :], in_=v_b.rearrange("(i p) -> i p", p=P))
+        nc.scalar.dma_start(out=bias_rows[0:CHUNKS, :], in_=v_b.rearrange("(k o) -> k o", k=CHUNKS))
         for first in range(0, PACK, STEP):
             nc.sync.dma_start(out=h_rows[:, first : first + STEP, :], in_=h_view[:, first : first + STEP, :])
         for first in range(0, N_BLOCKS, STEP):
@@ -80,15 +86,25 @@ def tile_soablock_pb_kernel(tc, attn, h_x, v_w_words, v_w_scales, v_b, x, out):
         scale_rows = v_w_scales[0].rearrange("(quadrant r) (k c) -> quadrant k r c", r=LIVE, k=PLANES)
         for quadrant in range(P // 32):
             nc.sync.dma_start(
-                out=w_planes[32 * quadrant : 32 * quadrant + PLANES * LIVE, :].bitcast(I32),
+                out=s_loaded[32 * quadrant : 32 * quadrant + PLANES * LIVE, :].bitcast(I32),
                 in_=scale_rows[quadrant].bitcast(I32),
             )
         nc.sync.dma_start(
-            out=w_words[:].bitcast(I32), in_=v_w_words[0].rearrange("p o t -> p (o t)").bitcast(I32)
+            out=w_loaded[:].bitcast(I32), in_=v_w_words[0].rearrange("p o t -> p (o t)").bitcast(I32)
         )
-        for first in range(0, O_TILES, X_TILES_PER_LOAD):
+        for first in range(0, TILES_PER_PLANE, X_TILES_PER_LOAD):
             tiles = slice(first, first + X_TILES_PER_LOAD)
             nc.sync.dma_start(out=x_rows[:, tiles, :], in_=x_view[:, tiles, :])
+        for k in range(1, CHUNKS):
+            tiles = slice(k * TILES_PER_PLANE, (k + 1) * TILES_PER_PLANE)
+            nc.sync.dma_start(out=x_rows[:, tiles, :], in_=x_chunks[:, k])
+
+        def order_words(k):
+            channels = slice(k * TILES_PER_PLANE * P, (k + 1) * TILES_PER_PLANE * P)
+            nc.vector.tensor_copy(
+                out=w_words[:, k - 1].bitcast(I32),
+                in_=w_loaded[:, channels].bitcast(I32).rearrange("p (r e) -> p e r", r=P),
+            )
 
         def flip(rows, grouped, first):
             for b in range(first, first + STEP):
@@ -138,22 +154,33 @@ def tile_soablock_pb_kernel(tc, attn, h_x, v_w_words, v_w_scales, v_b, x, out):
         for first in range(0, PACK, STEP):
             quantise(h_grouped, h_codes, h_scales, first)
 
-        bias_bank = banks.tile([P, P], BF16, tag="bank")
-        nc.tensor.transpose(bias_bank[:], bias_rows[:], ident_bf16[:])
-        nc.vector.tensor_copy(out=bias[:], in_=bias_bank[:, 0:O_TILES])
+        bias_bank = banks.tile([P, 2 * TILES_PER_PLANE, P], BF16, tag="bank")
+        for i in range(TILES_PER_PLANE):
+            nc.tensor.transpose(bias_bank[:, i, :], bias_rows[:, i * P : (i + 1) * P], ident_bf16[:])
+        for e in range(TILES_PER_PLANE):
+            nc.tensor.transpose(
+                bias_bank[:, TILES_PER_PLANE + e, :], bias_rows[:, e : C_OUT // CHUNKS : TILES_PER_PLANE], ident_bf16[:]
+            )
+        nc.vector.tensor_copy(out=bias[:, 0:TILES_PER_PLANE], in_=bias_bank[:, 0:TILES_PER_PLANE, 0])
+        nc.vector.tensor_copy(
+            out=bias[:, TILES_PER_PLANE:O_TILES].rearrange("p (k e) -> p k e", e=TILES_PER_PLANE),
+            in_=bias_bank[:, TILES_PER_PLANE : 2 * TILES_PER_PLANE, 1:CHUNKS].rearrange("p e k -> p k e"),
+        )
 
         def produce(i, half):
-            channels = slice(i * P, (i + 1) * P)
-            plane_top = LIVE * (i // TILES_PER_PLANE)
-            plane_cols = slice((i % TILES_PER_PLANE) * P, (i % TILES_PER_PLANE + 1) * P)
+            k, e = divmod(i, TILES_PER_PLANE)
+            if k == 0:
+                weight, weight_scales = w_loaded[:, i * P : (i + 1) * P], s_loaded[:, i * P : (i + 1) * P]
+            else:
+                weight, weight_scales = w_words[:, k - 1, e, :], w_planes[LIVE * k : P, e, :]
             cols = slice(half * N_HALF, (half + 1) * N_HALF)
             y_bank = banks.tile([P, N_HALF], F32, tag="bank")
             y_by_n = y_bank[:].rearrange("p (c r) -> p r c", r=P)
             out_by_n = out_rows[:, i, cols].rearrange("p (r c) -> p r c", r=P)
             nc.tensor.matmul_mx(
                 out=y_bank[:],
-                lhsT=w_words[:, channels].bitcast(FP8X4),
-                lhsT_scale=w_planes[plane_top:P, plane_cols],
+                lhsT=weight.bitcast(FP8X4),
+                lhsT_scale=weight_scales,
                 rhs=z_codes[:, cols].bitcast(FP8X4),
                 rhs_scale=z_scales[:, cols],
                 start=True,
@@ -192,11 +219,20 @@ def tile_soablock_pb_kernel(tc, attn, h_x, v_w_words, v_w_scales, v_b, x, out):
                 quantise_z(N_BLOCKS - STEP)
             produce(i, 0)
             store_half(i, 0)
+        nc.vector.tensor_copy(out=w_planes[:], in_=s_loaded[:].rearrange("p (r e) -> p e r", r=P))
+        order_words(1)
         for i in range(EARLY):
             produce(i, 1)
             store_half(i, 1)
 
         for i in range(EARLY, O_TILES):
+            k, e = divmod(i, TILES_PER_PLANE)
+            if e == 0 and k + 1 < CHUNKS:
+                order_words(k + 1)
             for half in range(HALVES):
                 produce(i, half)
-            nc.sync.dma_start(out=out_view[:, i, :], in_=out_rows[:, i, :])
+            if e % OUT_TILES_PER_STORE == OUT_TILES_PER_STORE - 1:
+                nc.sync.dma_start(
+                    out=out_chunks[:, k, e + 1 - OUT_TILES_PER_STORE : e + 1],
+                    in_=out_rows[:, i + 1 - OUT_TILES_PER_STORE : i + 1, :],
+                )

@@ -50,7 +50,8 @@ def tile_soablock_pb_kernel(tc, attn, h_x, v_w_words, v_w_scales, v_b, x, out):
         w_planes = keep.tile([P, TILES_PER_PLANE, P], U8, align_bytes=64)
         x_rows = keep.tile([P, O_TILES, POSITIONS], BF16)
         out_rows = keep.tile([P, O_TILES, POSITIONS], F32)
-        bias_rows = keep.tile([P, C_OUT // CHUNKS], BF16)
+        bias_rows = keep.tile([P, P], BF16)
+        bias_chunks = keep.tile([P, C_OUT // CHUNKS], BF16)
         bias = keep.tile([P, O_TILES], F32)
         ident = keep.tile([P, P], F32)
         ident_bf16 = keep.tile([P, P], BF16)
@@ -73,11 +74,13 @@ def tile_soablock_pb_kernel(tc, attn, h_x, v_w_words, v_w_scales, v_b, x, out):
         out_chunks = out[0].rearrange("(k p e) h w -> p k e (h w)", k=CHUNKS, p=P)
 
         nc.vector.memset(bias_rows[:], 0.0)
+        nc.vector.memset(bias_chunks[:], 0.0)
         nc.vector.memset(s_loaded[:].bitcast(I32), 0)
         make_identity(nc, ident[:])
         make_identity(nc, ident_bf16[:])
 
-        nc.scalar.dma_start(out=bias_rows[0:CHUNKS, :], in_=v_b.rearrange("(k o) -> k o", k=CHUNKS))
+        nc.scalar.dma_start(out=bias_rows[0:O_TILES, :], in_=v_b.rearrange("(i p) -> i p", p=P))
+        nc.scalar.dma_start(out=bias_chunks[0:CHUNKS, :], in_=v_b.rearrange("(k o) -> k o", k=CHUNKS))
         for first in range(0, PACK, STEP):
             nc.sync.dma_start(out=h_rows[:, first : first + STEP, :], in_=h_view[:, first : first + STEP, :])
         for first in range(0, N_BLOCKS, STEP):
@@ -154,18 +157,20 @@ def tile_soablock_pb_kernel(tc, attn, h_x, v_w_words, v_w_scales, v_b, x, out):
         for first in range(0, PACK, STEP):
             quantise(h_grouped, h_codes, h_scales, first)
 
-        bias_bank = banks.tile([P, 2 * TILES_PER_PLANE, P], BF16, tag="bank")
-        for i in range(TILES_PER_PLANE):
-            nc.tensor.transpose(bias_bank[:, i, :], bias_rows[:, i * P : (i + 1) * P], ident_bf16[:])
-        for e in range(TILES_PER_PLANE):
-            nc.tensor.transpose(
-                bias_bank[:, TILES_PER_PLANE + e, :], bias_rows[:, e : C_OUT // CHUNKS : TILES_PER_PLANE], ident_bf16[:]
+        bias_bank = banks.tile([P, P], BF16, tag="bank")
+        nc.tensor.transpose(bias_bank[:], bias_rows[:], ident_bf16[:])
+        nc.vector.tensor_copy(out=bias[:, 0:TILES_PER_PLANE], in_=bias_bank[:, 0:TILES_PER_PLANE])
+
+        def later_bias():
+            chunk_bank = banks.tile([P, TILES_PER_PLANE, P], BF16, tag="bank")
+            for e in range(TILES_PER_PLANE):
+                nc.tensor.transpose(
+                    chunk_bank[:, e, :], bias_chunks[:, e : C_OUT // CHUNKS : TILES_PER_PLANE], ident_bf16[:]
+                )
+            nc.vector.tensor_copy(
+                out=bias[:, TILES_PER_PLANE:O_TILES].rearrange("p (k e) -> p k e", e=TILES_PER_PLANE),
+                in_=chunk_bank[:, :, 1:CHUNKS].rearrange("p e k -> p k e"),
             )
-        nc.vector.tensor_copy(out=bias[:, 0:TILES_PER_PLANE], in_=bias_bank[:, 0:TILES_PER_PLANE, 0])
-        nc.vector.tensor_copy(
-            out=bias[:, TILES_PER_PLANE:O_TILES].rearrange("p (k e) -> p k e", e=TILES_PER_PLANE),
-            in_=bias_bank[:, TILES_PER_PLANE : 2 * TILES_PER_PLANE, 1:CHUNKS].rearrange("p e k -> p k e"),
-        )
 
         def produce(i, half):
             k, e = divmod(i, TILES_PER_PLANE)
@@ -214,16 +219,18 @@ def tile_soablock_pb_kernel(tc, attn, h_x, v_w_words, v_w_scales, v_b, x, out):
             if first >= 2 * STEP:
                 quantise_z(first - 2 * STEP)
 
+        nc.vector.tensor_copy(out=w_planes[:], in_=s_loaded[:].rearrange("p (r e) -> p e r", r=P))
+        order_words(1)
+
         for i in range(EARLY):
             if i == EARLY // 2:
                 quantise_z(N_BLOCKS - STEP)
             produce(i, 0)
             store_half(i, 0)
-        nc.vector.tensor_copy(out=w_planes[:], in_=s_loaded[:].rearrange("p (r e) -> p e r", r=P))
-        order_words(1)
         for i in range(EARLY):
             produce(i, 1)
             store_half(i, 1)
+        later_bias()
 
         for i in range(EARLY, O_TILES):
             k, e = divmod(i, TILES_PER_PLANE)
@@ -231,7 +238,9 @@ def tile_soablock_pb_kernel(tc, attn, h_x, v_w_words, v_w_scales, v_b, x, out):
                 order_words(k + 1)
             for half in range(HALVES):
                 produce(i, half)
-            if e % OUT_TILES_PER_STORE == OUT_TILES_PER_STORE - 1:
+            if i < EARLY + OUT_TILES_PER_STORE:
+                nc.sync.dma_start(out=out_chunks[:, k, e], in_=out_rows[:, i, :])
+            elif e % OUT_TILES_PER_STORE == OUT_TILES_PER_STORE - 1:
                 nc.sync.dma_start(
                     out=out_chunks[:, k, e + 1 - OUT_TILES_PER_STORE : e + 1],
                     in_=out_rows[:, i + 1 - OUT_TILES_PER_STORE : i + 1, :],

@@ -30,6 +30,7 @@ TILES_PER_PLANE = O_TILES // PLANES
 CHUNKS = PLANES
 X_TILES_PER_LOAD = 2
 OUT_TILES_PER_STORE = 2
+WARM_UP = 4
 EARLY = 4
 
 FLOPS = 2 * MID * POSITIONS * POSITIONS + 2 * C_OUT * MID * POSITIONS
@@ -55,6 +56,7 @@ def tile_soablock_pb_kernel(tc, attn, h_x, v_w_words, v_w_scales, v_b, x, out):
         bias = keep.tile([P, O_TILES], F32)
         ident = keep.tile([P, P], F32)
         ident_bf16 = keep.tile([P, P], BF16)
+        zeros = keep.tile([P, N_HALF], BF16)
 
         h_grouped = keep.tile([P, PACK, PASSES, P, PACK], BF16, align_bytes=64)
         a_grouped = keep.tile([P, N_BLOCKS, PASSES, P, PACK], BF16, align_bytes=64)
@@ -73,6 +75,7 @@ def tile_soablock_pb_kernel(tc, attn, h_x, v_w_words, v_w_scales, v_b, x, out):
         x_chunks = x[0].rearrange("(k p e) h w -> p k e (h w)", k=CHUNKS, p=P)
         out_chunks = out[0].rearrange("(k p e) h w -> p k e (h w)", k=CHUNKS, p=P)
 
+        nc.vector.memset(zeros[:], 0.0)
         nc.vector.memset(bias_rows[:], 0.0)
         nc.vector.memset(bias_chunks[:], 0.0)
         nc.vector.memset(s_loaded[:].bitcast(I32), 0)
@@ -109,10 +112,19 @@ def tile_soablock_pb_kernel(tc, attn, h_x, v_w_words, v_w_scales, v_b, x, out):
                 in_=w_loaded[:, channels].bitcast(I32).rearrange("p (r e) -> p e r", r=P),
             )
 
-        def flip(rows, grouped, first):
+        def flip(rows, grouped, first, warm=False):
             for b in range(first, first + STEP):
                 words = rows[:, b, :].bitcast(F32)
                 flipped = banks.tile([P, PASSES, PAIR, P], F32, tag="bank")
+                if warm and b == first:
+                    for k in range(WARM_UP):
+                        nc.tensor.matmul(
+                            out=flipped[:].rearrange("p g u r -> p (g u r)"),
+                            lhsT=zeros[:, 0:P],
+                            rhs=zeros[:],
+                            start=True,
+                            stop=True,
+                        )
                 for g in range(PASSES):
                     for u in range(PAIR):
                         first_word = (PAIR * g + u) * P
@@ -153,7 +165,7 @@ def tile_soablock_pb_kernel(tc, attn, h_x, v_w_words, v_w_scales, v_b, x, out):
             )
 
         for first in range(0, PACK, STEP):
-            flip(h_rows, h_grouped, first)
+            flip(h_rows, h_grouped, first, warm=(first == 0))
         for first in range(0, PACK, STEP):
             quantise(h_grouped, h_codes, h_scales, first)
 

@@ -76,14 +76,14 @@ def tile_soablock_pb_kernel(tc, attn, h_x, v_w_words, v_w_scales, v_b, x, out):
         out_chunks = out[0].rearrange("(k p e) h w -> p k e (h w)", k=CHUNKS, p=P)
 
         nc.vector.memset(zeros[:], 0.0)
-        nc.vector.memset(bias_rows[:], 0.0)
-        nc.vector.memset(bias_chunks[:], 0.0)
         nc.vector.memset(s_loaded[:].bitcast(I32), 0)
         make_identity(nc, ident[:])
         make_identity(nc, ident_bf16[:])
+        nc.gpsimd.memset(bias_rows[:], 0.0)
+        nc.gpsimd.memset(bias_chunks[:], 0.0)
+        nc.gpsimd.dma_start(out=bias_rows[0:O_TILES, :], in_=v_b.rearrange("(i p) -> i p", p=P))
+        nc.gpsimd.dma_start(out=bias_chunks[0:CHUNKS, :], in_=v_b.rearrange("(k o) -> k o", k=CHUNKS))
 
-        nc.scalar.dma_start(out=bias_rows[0:O_TILES, :], in_=v_b.rearrange("(i p) -> i p", p=P))
-        nc.scalar.dma_start(out=bias_chunks[0:CHUNKS, :], in_=v_b.rearrange("(k o) -> k o", k=CHUNKS))
         for first in range(0, PACK, STEP):
             nc.sync.dma_start(out=h_rows[:, first : first + STEP, :], in_=h_view[:, first : first + STEP, :])
         for first in range(0, N_BLOCKS, STEP):
@@ -169,20 +169,11 @@ def tile_soablock_pb_kernel(tc, attn, h_x, v_w_words, v_w_scales, v_b, x, out):
         for first in range(0, PACK, STEP):
             quantise(h_grouped, h_codes, h_scales, first)
 
-        bias_bank = banks.tile([P, P], BF16, tag="bank")
-        nc.tensor.transpose(bias_bank[:], bias_rows[:], ident_bf16[:])
-        nc.vector.tensor_copy(out=bias[:, 0:TILES_PER_PLANE], in_=bias_bank[:, 0:TILES_PER_PLANE])
+        def first_bias():
+            bias_bank = banks.tile([P, P], BF16, tag="bank")
+            nc.tensor.transpose(bias_bank[:], bias_rows[:], ident_bf16[:])
+            nc.vector.tensor_copy(out=bias[:, 0:TILES_PER_PLANE], in_=bias_bank[:, 0:TILES_PER_PLANE])
 
-        def later_bias():
-            chunk_bank = banks.tile([P, TILES_PER_PLANE, P], BF16, tag="bank")
-            for e in range(TILES_PER_PLANE):
-                nc.tensor.transpose(
-                    chunk_bank[:, e, :], bias_chunks[:, e : C_OUT // CHUNKS : TILES_PER_PLANE], ident_bf16[:]
-                )
-            nc.vector.tensor_copy(
-                out=bias[:, TILES_PER_PLANE:O_TILES].rearrange("p (k e) -> p k e", e=TILES_PER_PLANE),
-                in_=chunk_bank[:, :, 1:CHUNKS].rearrange("p e k -> p k e"),
-            )
 
         def produce(i, half):
             k, e = divmod(i, TILES_PER_PLANE)
@@ -226,6 +217,8 @@ def tile_soablock_pb_kernel(tc, attn, h_x, v_w_words, v_w_scales, v_b, x, out):
             if first < N_BLOCKS:
                 flip(a_rows, a_grouped, first)
                 quantise(a_grouped, a_codes, a_scales, first)
+            if first == N_BLOCKS // 2:
+                first_bias()
             if STEP <= first:
                 multiply(first - STEP)
             if first >= 2 * STEP:
@@ -239,10 +232,18 @@ def tile_soablock_pb_kernel(tc, attn, h_x, v_w_words, v_w_scales, v_b, x, out):
                 quantise_z(N_BLOCKS - STEP)
             produce(i, 0)
             store_half(i, 0)
+        chunk_bank = banks.tile([P, TILES_PER_PLANE, P], BF16, tag="bank")
+        for e in range(TILES_PER_PLANE):
+            nc.tensor.transpose(
+                chunk_bank[:, e, :], bias_chunks[:, e : C_OUT // CHUNKS : TILES_PER_PLANE], ident_bf16[:]
+            )
         for i in range(EARLY):
             produce(i, 1)
             store_half(i, 1)
-        later_bias()
+        nc.vector.tensor_copy(
+            out=bias[:, TILES_PER_PLANE:O_TILES].rearrange("p (k e) -> p k e", e=TILES_PER_PLANE),
+            in_=chunk_bank[:, :, 1:CHUNKS].rearrange("p e k -> p k e"),
+        )
 
         for i in range(EARLY, O_TILES):
             k, e = divmod(i, TILES_PER_PLANE)

@@ -237,24 +237,31 @@ def tile_soablock_pb_kernel(tc, attn, h_x, v_w_words, v_w_scales, v_b, x, out):
             nc.tensor.transpose(
                 chunk_bank[:, e, :], bias_chunks[:, e : C_OUT // CHUNKS : TILES_PER_PLANE], ident_bf16[:]
             )
-        for i in range(EARLY):
+        for i in range(1, EARLY, 2):
             produce(i, 1)
+        for i in range(0, EARLY, 2):
+            produce(i, 1)
+            store_half(i, 1)
+        for i in range(1, EARLY, 2):
             store_half(i, 1)
         nc.vector.tensor_copy(
             out=bias[:, TILES_PER_PLANE:O_TILES].rearrange("p (k e) -> p k e", e=TILES_PER_PLANE),
             in_=chunk_bank[:, :, 1:CHUNKS].rearrange("p e k -> p k e"),
         )
 
-        for i in range(EARLY, O_TILES):
+        for i in range(EARLY, O_TILES, OUT_TILES_PER_STORE):
             k, e = divmod(i, TILES_PER_PLANE)
             if e == 0 and k + 1 < CHUNKS:
                 order_words(k + 1)
-            for half in range(HALVES):
-                produce(i, half)
-            if i < EARLY + OUT_TILES_PER_STORE:
+            produce(i + 1, 1)
+            produce(i, 0)
+            produce(i, 1)
+            if i == EARLY:
                 nc.sync.dma_start(out=out_chunks[:, k, e], in_=out_rows[:, i, :])
-            elif e % OUT_TILES_PER_STORE == OUT_TILES_PER_STORE - 1:
+            produce(i + 1, 0)
+            if i == EARLY:
+                nc.sync.dma_start(out=out_chunks[:, k, e + 1], in_=out_rows[:, i + 1, :])
+            else:
                 nc.sync.dma_start(
-                    out=out_chunks[:, k, e + 1 - OUT_TILES_PER_STORE : e + 1],
-                    in_=out_rows[:, i + 1 - OUT_TILES_PER_STORE : i + 1, :],
+                    out=out_chunks[:, k, e : e + OUT_TILES_PER_STORE], in_=out_rows[:, i : i + OUT_TILES_PER_STORE, :]
                 )

from contextlib import ExitStack

import concourse.mybir as mybir
from concourse.masks import make_identity

F32 = mybir.dt.float32
BF16 = mybir.dt.bfloat16
I32 = mybir.dt.int32
U32 = mybir.dt.uint32
U8 = mybir.dt.uint8
FP8X4 = mybir.dt.float8_e4m3fn_x4
ADD = mybir.AluOpType.add
IDENTITY = mybir.ActivationFunctionType.Identity

P = 128
PACK = 4
PAIR = 2
POSITIONS = 1024
MID = 512
C_OUT = 2048
PASSES = POSITIONS // (P * PACK)
N_BLOCKS = POSITIONS // P
STEP = 2
N_HALF = 512
HALVES = POSITIONS // N_HALF
O_TILES = C_OUT // P
LIVE = 4
PLANES = 4
TILES_PER_PLANE = O_TILES // PLANES
CHUNKS = PLANES
X_TILES_PER_LOAD = 2
OUT_TILES_PER_STORE = 2
WARM_UP = 4
EARLY = 4

FLOPS = 2 * MID * POSITIONS * POSITIONS + 2 * C_OUT * MID * POSITIONS


def tile_soablock_pb_kernel(tc, attn, h_x, v_w_words, v_w_scales, v_b, x, out):
    nc = tc.nc
    with ExitStack() as ctx:
        keep = ctx.enter_context(tc.tile_pool(name="keep", bufs=1))
        banks = ctx.enter_context(tc.psum_pool(name="banks", bufs=8))
        ctx.enter_context(tc.manual_schedule())

        h_rows = keep.tile([P, PACK, POSITIONS], BF16)
        a_rows = keep.tile([P, N_BLOCKS, POSITIONS], BF16)
        w_loaded = keep.tile([P, C_OUT], U32, align_bytes=64)
        w_words = keep.tile([P, CHUNKS - 1, TILES_PER_PLANE, P], U32, align_bytes=64)
        s_loaded = keep.tile([P, C_OUT // PLANES], U8, align_bytes=64)
        w_planes = keep.tile([P, TILES_PER_PLANE, P], U8, align_bytes=64)
        x_rows = keep.tile([P, O_TILES, POSITIONS], BF16)
        out_rows = keep.tile([P, O_TILES, POSITIONS], F32)
        bias_rows = keep.tile([P, P], BF16)
        bias_chunks = keep.tile([P, C_OUT // CHUNKS], BF16)
        bias = keep.tile([P, O_TILES], F32)
        ident = keep.tile([P, P], F32)
        ident_bf16 = keep.tile([P, P], BF16)
        zeros = keep.tile([P, N_HALF], BF16)

        h_grouped = keep.tile([P, PACK, PASSES, P, PACK], BF16, align_bytes=64)
        a_grouped = keep.tile([P, N_BLOCKS, PASSES, P, PACK], BF16, align_bytes=64)
        z_grouped = keep.tile([P, POSITIONS, PACK], BF16, align_bytes=64)
        h_codes = keep.tile([P, PACK, PASSES, P], U32, align_bytes=64)
        h_scales = keep.tile([P, PACK, PASSES, P], U8, align_bytes=64)
        a_codes = keep.tile([P, N_BLOCKS, PASSES, P], U32, align_bytes=64)
        a_scales = keep.tile([P, N_BLOCKS, PASSES, P], U8, align_bytes=64)
        z_codes = keep.tile([P, POSITIONS], U32, align_bytes=64)
        z_scales = keep.tile([P, POSITIONS], U8, align_bytes=64)

        h_view = h_x[0].rearrange("(p t) m -> p t m", t=PACK)
        a_view = attn[0].rearrange("(half p c) m -> p half c m", half=HALVES, p=P)
        x_view = x[0].rearrange("(i p) h w -> p i (h w)", p=P)
        out_view = out[0].rearrange("(i p) h w -> p i (h w)", p=P)
        x_chunks = x[0].rearrange("(k p e) h w -> p k e (h w)", k=CHUNKS, p=P)
        out_chunks = out[0].rearrange("(k p e) h w -> p k e (h w)", k=CHUNKS, p=P)

        nc.vector.memset(zeros[:], 0.0)
        nc.vector.memset(s_loaded[:].bitcast(I32), 0)
        make_identity(nc, ident[:])
        make_identity(nc, ident_bf16[:])
        nc.gpsimd.memset(bias_rows[:], 0.0)
        nc.gpsimd.memset(bias_chunks[:], 0.0)
        nc.gpsimd.dma_start(out=bias_rows[0:O_TILES, :], in_=v_b.rearrange("(i p) -> i p", p=P))
        nc.gpsimd.dma_start(out=bias_chunks[0:CHUNKS, :], in_=v_b.rearrange("(k o) -> k o", k=CHUNKS))

        for first in range(0, PACK, STEP):
            nc.sync.dma_start(out=h_rows[:, first : first + STEP, :], in_=h_view[:, first : first + STEP, :])
        for first in range(0, N_BLOCKS, STEP):
            half, c = divmod(first, N_BLOCKS // HALVES)
            nc.sync.dma_start(out=a_rows[:, first : first + STEP, :], in_=a_view[:, half, c : c + STEP, :])
        scale_rows = v_w_scales[0].rearrange("(quadrant r) (k c) -> quadrant k r c", r=LIVE, k=PLANES)
        for quadrant in range(P // 32):
            nc.sync.dma_start(
                out=s_loaded[32 * quadrant : 32 * quadrant + PLANES * LIVE, :].bitcast(I32),
                in_=scale_rows[quadrant].bitcast(I32),
            )
        nc.sync.dma_start(
            out=w_loaded[:].bitcast(I32), in_=v_w_words[0].rearrange("p o t -> p (o t)").bitcast(I32)
        )
        for first in range(0, TILES_PER_PLANE, X_TILES_PER_LOAD):
            tiles = slice(first, first + X_TILES_PER_LOAD)
            nc.sync.dma_start(out=x_rows[:, tiles, :], in_=x_view[:, tiles, :])
        for k in range(1, CHUNKS):
            tiles = slice(k * TILES_PER_PLANE, (k + 1) * TILES_PER_PLANE)
            nc.sync.dma_start(out=x_rows[:, tiles, :], in_=x_chunks[:, k])

        def order_words(k):
            channels = slice(k * TILES_PER_PLANE * P, (k + 1) * TILES_PER_PLANE * P)
            nc.vector.tensor_copy(
                out=w_words[:, k - 1].bitcast(I32),
                in_=w_loaded[:, channels].bitcast(I32).rearrange("p (r e) -> p e r", r=P),
            )

        def flip(rows, grouped, first, warm=False):
            for b in range(first, first + STEP):
                words = rows[:, b, :].bitcast(F32)
                flipped = banks.tile([P, PASSES, PAIR, P], F32, tag="bank")
                if warm and b == first:
                    for k in range(WARM_UP):
                        nc.tensor.matmul(
                            out=flipped[:].rearrange("p g u r -> p (g u r)"),
                            lhsT=zeros[:, 0:P],
                            rhs=zeros[:],
                            start=True,
                            stop=True,
                        )
                for g in range(PASSES):
                    for u in range(PAIR):
                        first_word = (PAIR * g + u) * P
                        nc.tensor.transpose(flipped[:, g, u, :], words[:, first_word : first_word + P], ident[:])
                copy = nc.vector.tensor_copy if b % 2 == 0 else nc.scalar.copy
                copy(out=grouped[:, b].bitcast(F32), in_=flipped[:].rearrange("p g u r -> p g r u"))

        def quantise(grouped, codes, scales, first):
            blocks = slice(first, first + STEP)
            nc.vector.quantize_mx(
                out=codes[:, blocks].rearrange("p b g r -> p (b g r)").bitcast(FP8X4),
                scales=scales[:, blocks].rearrange("p b g r -> p (b g r)"),
                in_=grouped[:, blocks].rearrange("p b g r t -> p (b g r t)"),
            )

        def multiply(first):
            for j in range(first, first + STEP):
                z_bank = banks.tile([P, PACK, P], F32, tag="bank")
                for t in range(PACK):
                    for g in range(PASSES):
                        nc.tensor.matmul_mx(
                            out=z_bank[:, t, :],
                            lhsT=h_codes[:, t, g, :].bitcast(FP8X4),
                            lhsT_scale=h_scales[:, t, g, :],
                            rhs=a_codes[:, j, g, :].bitcast(FP8X4),
                            rhs_scale=a_scales[:, j, g, :],
                            start=(g == 0),
                            stop=(g == PASSES - 1),
                        )
                nc.scalar.copy(out=z_grouped[:, j * P : (j + 1) * P, :], in_=z_bank[:].rearrange("p t r -> p r t"))

        def quantise_z(first):
            cols = slice(first * P, (first + STEP) * P)
            nc.vector.quantize_mx(
                out=z_codes[:, cols].bitcast(FP8X4),
                scales=z_scales[:, cols],
                in_=z_grouped[:, cols, :].rearrange("p n t -> p (n t)"),
            )

        for first in range(0, PACK, STEP):
            flip(h_rows, h_grouped, first, warm=(first == 0))
        for first in range(0, PACK, STEP):
            quantise(h_grouped, h_codes, h_scales, first)

        def first_bias():
            bias_bank = banks.tile([P, P], BF16, tag="bank")
            nc.tensor.transpose(bias_bank[:], bias_rows[:], ident_bf16[:])
            nc.vector.tensor_copy(out=bias[:, 0:TILES_PER_PLANE], in_=bias_bank[:, 0:TILES_PER_PLANE])


        def produce(i, half):
            k, e = divmod(i, TILES_PER_PLANE)
            if k == 0:
                weight, weight_scales = w_loaded[:, i * P : (i + 1) * P], s_loaded[:, i * P : (i + 1) * P]
            else:
                weight, weight_scales = w_words[:, k - 1, e, :], w_planes[LIVE * k : P, e, :]
            cols = slice(half * N_HALF, (half + 1) * N_HALF)
            y_bank = banks.tile([P, N_HALF], F32, tag="bank")
            y_by_n = y_bank[:].rearrange("p (c r) -> p r c", r=P)
            out_by_n = out_rows[:, i, cols].rearrange("p (r c) -> p r c", r=P)
            nc.tensor.matmul_mx(
                out=y_bank[:],
                lhsT=weight.bitcast(FP8X4),
                lhsT_scale=weight_scales,
                rhs=z_codes[:, cols].bitcast(FP8X4),
                rhs_scale=z_scales[:, cols],
                start=True,
                stop=True,
            )
            if i % 2 == 1 and half == 1:
                nc.scalar.activation(out=out_by_n, in_=y_by_n, func=IDENTITY, bias=bias[:, i : i + 1])
                nc.gpsimd.tensor_tensor(
                    out=out_rows[:, i, cols], in0=out_rows[:, i, cols], in1=x_rows[:, i, cols], op=ADD
                )
            else:
                nc.vector.scalar_tensor_tensor(
                    out=out_by_n,
                    in0=y_by_n,
                    scalar=bias[:, i : i + 1],
                    in1=x_rows[:, i, cols].rearrange("p (r c) -> p r c", r=P),
                    op0=ADD,
                    op1=ADD,
                )

        def store_half(i, half):
            cols = slice(half * N_HALF, (half + 1) * N_HALF)
            nc.sync.dma_start(out=out_view[:, i, cols], in_=out_rows[:, i, cols])

        for first in range(0, N_BLOCKS + STEP, STEP):
            if first < N_BLOCKS:
                flip(a_rows, a_grouped, first)
                quantise(a_grouped, a_codes, a_scales, first)
            if first == N_BLOCKS // 2:
                first_bias()
            if STEP <= first:
                multiply(first - STEP)
            if first >= 2 * STEP:
                quantise_z(first - 2 * STEP)

        nc.vector.tensor_copy(out=w_planes[:], in_=s_loaded[:].rearrange("p (r e) -> p e r", r=P))
        order_words(1)

        for i in range(EARLY):
            if i == EARLY // 2:
                quantise_z(N_BLOCKS - STEP)
            produce(i, 0)
            store_half(i, 0)
        chunk_bank = banks.tile([P, TILES_PER_PLANE, P], BF16, tag="bank")
        for e in range(TILES_PER_PLANE):
            nc.tensor.transpose(
                chunk_bank[:, e, :], bias_chunks[:, e : C_OUT // CHUNKS : TILES_PER_PLANE], ident_bf16[:]
            )
        for i in range(1, EARLY, 2):
            produce(i, 1)
        for i in range(0, EARLY, 2):
            produce(i, 1)
            store_half(i, 1)
        for i in range(1, EARLY, 2):
            store_half(i, 1)
        nc.vector.tensor_copy(
            out=bias[:, TILES_PER_PLANE:O_TILES].rearrange("p (k e) -> p k e", e=TILES_PER_PLANE),
            in_=chunk_bank[:, :, 1:CHUNKS].rearrange("p e k -> p k e"),
        )

        for i in range(EARLY, O_TILES, OUT_TILES_PER_STORE):
            k, e = divmod(i, TILES_PER_PLANE)
            if e == 0 and k + 1 < CHUNKS:
                order_words(k + 1)
            produce(i + 1, 1)
            produce(i, 0)
            produce(i, 1)
            if i == EARLY:
                nc.sync.dma_start(out=out_chunks[:, k, e], in_=out_rows[:, i, :])
            produce(i + 1, 0)
            if i == EARLY:
                nc.sync.dma_start(out=out_chunks[:, k, e + 1], in_=out_rows[:, i + 1, :])
            else:
                nc.sync.dma_start(
                    out=out_chunks[:, k, e : e + OUT_TILES_PER_STORE], in_=out_rows[:, i : i + OUT_TILES_PER_STORE, :]
                )
